import numpy as np
import ml_dtypes


def mxq(x, axis, fmt="e4m3"):
    dtype, down = {"e4m3": (ml_dtypes.float8_e4m3fn, 7), "e5m2": (ml_dtypes.float8_e5m2, 14)}[fmt]
    v = np.moveaxis(np.asarray(x, np.float32).astype(ml_dtypes.bfloat16).astype(np.float64), axis, -1)
    blocks = v.reshape(v.shape[:-1] + (-1, 32))
    amax = np.abs(blocks).max(-1, keepdims=True)
    byte = np.maximum(np.where(amax > 0, np.frexp(amax)[1] - 1 + 127, 0) - down, 1)
    scale = np.exp2(byte - 127.0)
    codes = (blocks / scale).astype(np.float32).astype(dtype).astype(np.float64)
    return np.moveaxis((codes * scale).reshape(v.shape), -1, axis)


WIDE = False


def mx_kscale(k):
    if not WIDE:
        return np.ones(k)
    levels = np.array([10, -10, 5, -5, 0])
    a = np.random.permutation(np.resize(levels, k // 512 * 4)).reshape(k // 512, 4)
    idx = np.arange(k)
    return np.exp2(a[idx // 512, idx % 128 // 32])


BF16 = ml_dtypes.bfloat16


def bf(x):
    return np.asarray(x, np.float32).astype(BF16)


def f64(x):
    return np.asarray(x).astype(np.float64)


B, S, E, H, KV, HD, HID = 2, 256, 1024, 8, 4, 128, 3072
F = (H + 2 * KV) * HD
EPS = 1e-6
ROPE_BASE = 1000000.0


def rmsnorm(v, w):
    var = np.mean(v * v, axis=-1, keepdims=True)
    return v * (1.0 / np.sqrt(var + EPS)) * w


def apply_rope(v, cos, sin):
    v1 = v[..., 0::2]
    v2 = v[..., 1::2]
    r1 = v1 * cos - v2 * sin
    r2 = v1 * sin + v2 * cos
    return np.stack([r1, r2], axis=-1).reshape(v.shape)


def setup_inputs():
    s = mx_kscale(E)
    return {"x": bf(np.random.standard_normal((B, S, E)) * 2.0),
            "ln_w": bf((1.0 + 0.1 * np.random.standard_normal(E)) * s),
            "qkv_w": bf(np.random.standard_normal((E, F)) * 2.0 / np.sqrt(E) / s[:, None]),
            "q_norm_w": bf(1.0 + 0.1 * np.random.standard_normal(HD)),
            "k_norm_w": bf(1.0 + 0.1 * np.random.standard_normal(HD))}


def reference(x, ln_w, qkv_w, q_norm_w, k_norm_w):
    h = rmsnorm(f64(x), f64(ln_w))
    qkv = mxq(h, 2, "e4m3") @ mxq(f64(qkv_w), 0, "e4m3")
    q = qkv[..., : H * HD].reshape(B, S, H, HD)
    k = qkv[..., H * HD : (H + KV) * HD].reshape(B, S, KV, HD)
    v = qkv[..., (H + KV) * HD :].reshape(B, S, KV, HD)
    q = rmsnorm(q, f64(q_norm_w))
    k = rmsnorm(k, f64(k_norm_w))
    pos = np.arange(S, dtype=np.float64)
    inv_freq = 1.0 / (ROPE_BASE ** (np.arange(0, HD, 2, dtype=np.float64) / HD))
    ang = pos[:, None] * inv_freq
    cos = np.cos(ang)[None, :, None, :]
    sin = np.sin(ang)[None, :, None, :]
    return apply_rope(q, cos, sin), apply_rope(k, cos, sin), v

@@ -1,0 +1,422 @@
+import math
+from contextlib import ExitStack
+
+import concourse.mybir as mybir
+from concourse.masks import make_identity
+
+F32 = mybir.dt.float32
+BF16 = mybir.dt.bfloat16
+I32 = mybir.dt.int32
+U32 = mybir.dt.uint32
+U8 = mybir.dt.uint8
+FP8X4 = mybir.dt.float8_e4m3fn_x4
+ALU = mybir.AluOpType
+ACT = mybir.ActivationFunctionType
+
+P = 128
+TOKENS = 512
+SEQ_TILES = 2
+MODEL = 1024
+FUSED = 2048
+HEAD = 128
+PAIRS = HEAD // 2
+PAIR_BITS = 6
+TOKEN_TILES = TOKENS // P
+CHUNK = 512
+CHUNKS = FUSED // CHUNK
+HEADS = CHUNK // HEAD
+PACK = 4
+PASS_ROWS = P * PACK
+PASSES = MODEL // PASS_ROWS
+PIECE = 256
+PIECES = CHUNK // PIECE
+EPS = 1e-6
+ROPE_BASE = 1000000.0
+KEYS = 2
+VALUES = 3
+FLOPS = 2 * TOKENS * MODEL * FUSED
+
+
+def tile_qwen3block_pa_kernel(tc, x, ln_w, qkv_w, q_norm_w, k_norm_w, out_0, out_1, out_2):
+    nc = tc.nc
+    x_rows = x.flatten_outer_dims()
+    queries = out_0.rearrange("b s h d -> (b s) (h d)")
+    keys = out_1.rearrange("b s h d -> (b s) (h d)")
+    values_out = out_2.rearrange("b s h d -> (b s) (h d)")
+    chunk_target = [(queries, 0, 0), (queries, CHUNK, 0), (keys, 0, 1), (values_out, 0, None)]
+
+    with ExitStack() as ctx:
+        const = ctx.enter_context(tc.tile_pool(name="const", bufs=1))
+        keep = ctx.enter_context(tc.tile_pool(name="keep", bufs=1))
+        unread = ctx.enter_context(tc.tile_pool(name="unread", bufs=2))
+        grouped_w = ctx.enter_context(tc.tile_pool(name="grouped_w", bufs=2))
+        stats = ctx.enter_context(tc.tile_pool(name="stats", bufs=8))
+        products_pool = ctx.enter_context(tc.tile_pool(name="products_pool", bufs=4))
+        results = ctx.enter_context(tc.tile_pool(name="results", bufs=8))
+        psum = ctx.enter_context(tc.psum_pool(name="psum", bufs=8))
+        ctx.enter_context(tc.manual_schedule())
+
+        gain_rows = const.tile([P, MODEL + 2 * HEAD], BF16)
+        ones = const.tile([P, P], BF16)
+        identity = const.tile([P, P], BF16)
+        eps_col = const.tile([P, 1], F32)
+        table_loads = const.tile([P, 2], F32)
+        position_int = const.tile([P, SEQ_TILES], I32)
+        position = const.tile([P, SEQ_TILES], F32)
+        inv_freq = const.tile([P, PAIRS], F32)
+        angle = const.tile([P, SEQ_TILES, PAIRS], F32)
+        turns_int = const.tile([P, SEQ_TILES, PAIRS], I32)
+        turns = const.tile([P, SEQ_TILES, PAIRS], F32)
+        partly_reduced = const.tile([P, SEQ_TILES, PAIRS], F32)
+        reduced = const.tile([P, SEQ_TILES, PAIRS], F32)
+        sines_uv = const.tile([P, 2, SEQ_TILES, PAIRS], F32)
+        sines_squared = const.tile([P, 2, SEQ_TILES, PAIRS], F32)
+        minus_two_cos = const.tile([P, SEQ_TILES, PAIRS], F32)
+        rotation = const.tile([P, SEQ_TILES, 2, PAIRS, 2], F32)
+        head_gain = const.tile([P, 2, HEAD], F32)
+        rope_table = const.tile([P, 2, SEQ_TILES * 2, HEAD], F32)
+        x_sumsq = const.tile([P, TOKEN_TILES], F32)
+        x_rstd_cols = const.tile([P, TOKEN_TILES], F32)
+        x_tile = {}
+        w_planes = {}
+        ln_w_psum = []
+        head_gain_psum = []
+        h_tile = {}
+        h_transposed = {}
+        h_grouped = {}
+        h_codes = {}
+        h_scales = {}
+        w_grouped = {}
+        w_codes = {}
+        w_scales = {}
+        bank = {}
+        head_sumsq = {}
+        head_rstd_cols = {}
+        pair_products = {}
+        result = {}
+
+        def constants():
+            nc.gpsimd.memset(eps_col[:], EPS)
+            nc.gpsimd.iota(position_int[:], pattern=[[P, SEQ_TILES]], base=0, channel_multiplier=1)
+            nc.gpsimd.memset(ones[:], 1.0)
+            make_identity(nc, identity[:])
+            nc.scalar.activation(out=table_loads[:, 0:1], in_=eps_col[:], func=ACT.Sin)
+
+        def zero_gain_rows():
+            nc.vector.memset(gain_rows[:].bitcast(I32), 0)
+
+        def angles():
+            nc.vector.tensor_copy(out=position[:], in_=position_int[:])
+            ratio = ROPE_BASE ** (-1.0 / PAIRS)
+            nc.vector.memset(inv_freq[:], 1.0)
+            for b in range(PAIR_BITS):
+                bit_set = inv_freq[:].rearrange("p (q t r) -> p q t r", t=2, r=2**b)[:, :, 1, :]
+                nc.vector.tensor_scalar(
+                    out=bit_set, in0=bit_set, scalar1=ratio ** (2**b), scalar2=None, op0=ALU.mult
+                )
+            for s in range(SEQ_TILES):
+                nc.vector.tensor_scalar(
+                    out=angle[:, s, :],
+                    in0=inv_freq[:],
+                    scalar1=position[:, s : s + 1],
+                    scalar2=-math.pi / 2.0,
+                    op0=ALU.mult,
+                    op1=ALU.add,
+                )
+            nc.vector.tensor_scalar(
+                out=turns_int[:], in0=angle[:], scalar1=1.0 / (2.0 * math.pi), scalar2=0.25, op0=ALU.mult, op1=ALU.add
+            )
+            nc.vector.tensor_copy(out=turns[:], in_=turns_int[:])
+            two_pi_high = 6.28125
+            two_pi_low = 2.0 * math.pi - two_pi_high
+            nc.vector.scalar_tensor_tensor(
+                out=partly_reduced[:], in0=turns[:], scalar=-two_pi_high, in1=angle[:], op0=ALU.mult, op1=ALU.add
+            )
+            nc.vector.scalar_tensor_tensor(
+                out=reduced[:], in0=turns[:], scalar=-two_pi_low, in1=partly_reduced[:], op0=ALU.mult, op1=ALU.add
+            )
+
+        def sines():
+            nc.scalar.activation(out=sines_uv[:, 0], in_=reduced[:], func=ACT.Sin, scale=0.5)
+            nc.scalar.activation(out=sines_uv[:, 1], in_=reduced[:], func=ACT.Sin, scale=0.25)
+
+        def load_rsqrt_table():
+            nc.scalar.activation(
+                out=table_loads[:, 1:2],
+                in_=sines_uv[:, 0, 0, 0:1],
+                func=ACT.Abs_reciprocal_sqrt,
+                bias=eps_col[:, 0:1],
+                scale=0.0,
+            )
+
+        def rotations():
+            u = sines_uv[:, 0]
+            nc.gpsimd.tensor_tensor(out=sines_squared[:], in0=sines_uv[:], in1=sines_uv[:], op=ALU.mult)
+            nc.gpsimd.tensor_scalar(
+                out=minus_two_cos[:], in0=sines_squared[:, 1], scalar1=4.0, scalar2=-2.0, op0=ALU.mult, op1=ALU.add
+            )
+            nc.gpsimd.tensor_tensor(out=rotation[:, :, 0, :, 0], in0=u, in1=minus_two_cos[:], op=ALU.mult)
+            nc.gpsimd.tensor_tensor(out=rotation[:, :, 1, :, 1], in0=u, in1=minus_two_cos[:], op=ALU.mult)
+            nc.gpsimd.tensor_scalar(
+                out=rotation[:, :, 0, :, 1], in0=sines_squared[:, 0], scalar1=2.0, scalar2=-1.0, op0=ALU.mult, op1=ALU.add
+            )
+            nc.gpsimd.tensor_scalar(
+                out=rotation[:, :, 1, :, 0], in0=sines_squared[:, 0], scalar1=-2.0, scalar2=1.0, op0=ALU.mult, op1=ALU.add
+            )
+
+        def load_x(a):
+            x_tile[a] = keep.tile([P, MODEL], BF16, name="x_tile%d" % a)
+            nc.sync.dma_start(out=x_tile[a][:], in_=x_rows[a * P : (a + 1) * P, :])
+
+        def load_gains():
+            nc.sync.dma_start(out=gain_rows[0:1, 0:MODEL], in_=ln_w.unsqueeze(0))
+            nc.sync.dma_start(out=gain_rows[0:1, MODEL : MODEL + HEAD], in_=q_norm_w.unsqueeze(0))
+            nc.sync.dma_start(out=gain_rows[0:1, MODEL + HEAD : MODEL + 2 * HEAD], in_=k_norm_w.unsqueeze(0))
+
+        def load_weights(c, g):
+            w_planes[(c, g)] = keep.tile([P, PACK, CHUNK], BF16, name="w_planes%d%d" % (c, g))
+            nc.sync.dma_start(
+                out=w_planes[(c, g)][:],
+                in_=qkv_w[g * PASS_ROWS : (g + 1) * PASS_ROWS, c * CHUNK : (c + 1) * CHUNK].rearrange(
+                    "(j p) n -> p j n", p=P
+                ),
+            )
+
+        def spread_gains():
+            for half in range(2):
+                spread = psum.tile([P, CHUNK], F32, tag="bank", name="ln_w_psum%d" % half)
+                nc.tensor.matmul(
+                    spread[:], lhsT=ones[:], rhs=gain_rows[:, half * CHUNK : (half + 1) * CHUNK], start=True, stop=True
+                )
+                ln_w_psum.append(spread)
+            spread = psum.tile([P, CHUNK], F32, tag="bank", name="head_gain_psum")
+            nc.tensor.matmul(
+                spread[:, 0 : 2 * HEAD], lhsT=ones[:], rhs=gain_rows[:, MODEL : MODEL + 2 * HEAD], start=True, stop=True
+            )
+            head_gain_psum.append(spread)
+
+        def copy_head_gains():
+            nc.scalar.copy(out=head_gain[:].rearrange("p w d -> p (w d)"), in_=head_gain_psum[0][:, 0 : 2 * HEAD])
+
+        def rope_tables():
+            for w in range(2):
+                nc.gpsimd.tensor_tensor(
+                    out=rope_table[:, w],
+                    in0=rotation[:].rearrange("p s e j m -> p (s e) (j m)"),
+                    in1=head_gain[:, w, :].unsqueeze(1).to_broadcast([P, SEQ_TILES * 2, HEAD]),
+                    op=ALU.mult,
+                )
+
+        def x_squares(a):
+            squares = unread.tile([P, MODEL], BF16, tag="x_squares")
+            nc.scalar.activation(out=squares[:], in_=x_tile[a][:], func=ACT.Square, accum_out=x_sumsq[:, a : a + 1])
+
+        def x_rstd(a):
+            nc.scalar.activation(
+                out=x_rstd_cols[:, a : a + 1],
+                in_=x_sumsq[:, a : a + 1],
+                func=ACT.Abs_reciprocal_sqrt,
+                bias=eps_col[:, 0:1],
+                scale=1.0 / MODEL,
+            )
+
+        def normalise(a):
+            h_tile[a] = keep.tile([P, MODEL], BF16, name="h_tile%d" % a)
+            for half in range(2):
+                cols = slice(half * CHUNK, (half + 1) * CHUNK)
+                nc.vector.scalar_tensor_tensor(
+                    out=h_tile[a][:, cols],
+                    in0=x_tile[a][:, cols],
+                    scalar=x_rstd_cols[:, a : a + 1],
+                    in1=ln_w_psum[half][:],
+                    op0=ALU.mult,
+                    op1=ALU.mult,
+                )
+
+        def transpose_h(a):
+            h_transposed[a] = psum.tile([P, MODEL], BF16, tag="bank", name="h_transposed%d" % a)
+            for block in range(MODEL // P):
+                cols = slice(block * P, (block + 1) * P)
+                nc.tensor.transpose(h_transposed[a][:, cols], h_tile[a][:, cols], identity[:])
+
+        def group_h(a):
+            h_grouped[a] = keep.tile([P, PASSES, P, PACK], BF16, name="h_grouped%d" % a, align_bytes=64)
+            nc.scalar.copy(
+                out=h_grouped[a][:], in_=h_transposed[a][:].rearrange("p (g j t) -> p g t j", g=PASSES, j=PACK)
+            )
+
+        def quantise_h(a):
+            h_codes[a] = keep.tile([P, PASSES * P], U32, name="h_codes%d" % a, align_bytes=64)
+            h_scales[a] = keep.tile([P, PASSES * P], U8, name="h_scales%d" % a, align_bytes=64)
+            nc.vector.quantize_mx(
+                out=h_codes[a][:].bitcast(FP8X4),
+                scales=h_scales[a][:],
+                in_=h_grouped[a][:].rearrange("p g t j -> p (g t j)"),
+            )
+
+        def regroup_weights(copy, c, g, piece):
+            if c not in w_grouped:
+                w_grouped[c] = grouped_w.tile(
+                    [P, PASSES, CHUNK, PACK], BF16, tag="w_grouped", name="w_grouped%d" % c, align_bytes=64
+                )
+            cols = slice(piece * PIECE, (piece + 1) * PIECE)
+            copy(
+                out=w_grouped[c][:, g, cols, :].rearrange("p (n i) j -> p n j i", i=4),
+                in_=w_planes[(c, g)][:, :, cols].rearrange("p j (n i) -> p n j i", i=4),
+            )
+
+        def quantise_weights(c):
+            w_codes[c] = keep.tile([P, PASSES, CHUNK], U32, name="w_codes%d" % c, align_bytes=64)
+            w_scales[c] = keep.tile([P, PASSES, CHUNK], U8, name="w_scales%d" % c, align_bytes=64)
+            nc.vector.quantize_mx(
+                out=w_codes[c][:].rearrange("p g n -> p (g n)").bitcast(FP8X4),
+                scales=w_scales[c][:].rearrange("p g n -> p (g n)"),
+                in_=w_grouped[c][:].rearrange("p g n j -> p (g n j)"),
+            )
+
+        def project(c, a):
+            bank[(c, a)] = psum.tile([P, CHUNK], F32, tag="bank", name="bank")
+            for g in range(PASSES):
+                tokens = slice(g * P, (g + 1) * P)
+                nc.tensor.matmul_mx(
+                    out=bank[(c, a)][:],
+                    lhsT=h_codes[a][:, tokens].bitcast(FP8X4),
+                    lhsT_scale=h_scales[a][:, tokens],
+                    rhs=w_codes[c][:, g, :].bitcast(FP8X4),
+                    rhs_scale=w_scales[c][:, g, :],
+                    start=(g == 0),
+                    stop=(g == PASSES - 1),
+                )
+
+        def head_squares(c, a):
+            head_sumsq[(c, a)] = stats.tile([P, HEADS], F32, tag="head_sumsq", name="head_sumsq")
+            for h in range(HEADS):
+                squares = unread.tile([P, HEAD], BF16, tag="head_squares")
+                nc.scalar.activation(
+                    out=squares[:],
+                    in_=bank[(c, a)][:, h * HEAD : (h + 1) * HEAD],
+                    func=ACT.Square,
+                    accum_out=head_sumsq[(c, a)][:, h : h + 1],
+                )
+
+        def head_rstd(c, a):
+            head_rstd_cols[(c, a)] = stats.tile([P, HEADS], F32, tag="head_rstd", name="head_rstd")
+            nc.scalar.activation(
+                out=head_rstd_cols[(c, a)][:],
+                in_=head_sumsq[(c, a)][:],
+                func=ACT.Abs_reciprocal_sqrt,
+                bias=eps_col[:, 0:1],
+                scale=1.0 / HEAD,
+            )
+
+        def rotation_products(c, a):
+            gain = chunk_target[c][2]
+            first = 2 * (a % SEQ_TILES)
+            pair_products[(c, a)] = products_pool.tile([P, HEADS, 2, HEAD], F32, tag="pair_products", name="pair_products")
+            for h in range(HEADS):
+                nc.vector.scalar_tensor_tensor(
+                    out=pair_products[(c, a)][:, h],
+                    in0=bank[(c, a)][:, h * HEAD : (h + 1) * HEAD].unsqueeze(1).to_broadcast([P, 2, HEAD]),
+                    scalar=head_rstd_cols[(c, a)][:, h : h + 1],
+                    in1=rope_table[:, gain, first : first + 2, :],
+                    op0=ALU.mult,
+                    op1=ALU.mult,
+                )
+
+        def add_products(c, a):
+            result[(c, a)] = results.tile([P, CHUNK], F32, tag="result", name="result")
+            by_m = pair_products[(c, a)][:].rearrange("p h e (j m) -> p h j e m", m=2)
+            nc.gpsimd.tensor_tensor(
+                out=result[(c, a)][:].rearrange("p (h j e) -> p h j e", h=HEADS, e=2),
+                in0=by_m[:, :, :, :, 0],
+                in1=by_m[:, :, :, :, 1],
+                op=ALU.add,
+            )
+
+        def copy_values(a):
+            result[(VALUES, a)] = results.tile([P, CHUNK], F32, tag="result", name="result")
+            nc.scalar.copy(out=result[(VALUES, a)][:], in_=bank[(VALUES, a)][:])
+
+        def store(c, a):
+            target, first_col, gain = chunk_target[c]
+            nc.sync.dma_start(out=target[a * P : (a + 1) * P, first_col : first_col + CHUNK], in_=result[(c, a)][:])
+
+        on_vector = nc.vector.tensor_copy
+        on_scalar = nc.scalar.copy
+        pieces = [(g, piece) for g in range(PASSES) for piece in range(PIECES)]
+
+        constants()
+        zero_gain_rows()
+        load_x(0)
+        load_gains()
+        load_weights(0, 0)
+        load_x(1)
+        load_weights(0, 1)
+        load_x(2)
+        load_x(3)
+        for c in range(1, CHUNKS):
+            for g in range(PASSES):
+                load_weights(c, g)
+        angles()
+
+        x_squares(0)
+        sines()
+        load_rsqrt_table()
+        rotations()
+        spread_gains()
+        for g, piece in pieces:
+            regroup_weights(on_vector, 0, g, piece)
+        x_rstd(0)
+        for a in range(1, TOKEN_TILES):
+            x_squares(a)
+            x_rstd(a)
+
+        last = TOKEN_TILES - 1
+        for a in range(last):
+            normalise(a)
+            transpose_h(a)
+        quantise_weights(0)
+        group_h(0)
+        quantise_h(0)
+        normalise(last)
+        transpose_h(last)
+        group_h(1)
+        quantise_h(1)
+        regroup_weights(on_vector, 1, *pieces[0])
+        group_h(2)
+        quantise_h(2)
+        copy_head_gains()
+        rope_tables()
+        regroup_weights(on_scalar, KEYS, *pieces[-1])
+        for g, piece in pieces[1:]:
+            regroup_weights(on_vector, 1, g, piece)
+        quantise_weights(1)
+        group_h(last)
+        quantise_h(last)
+
+        key_steps_from = KEYS * TOKEN_TILES - 2 - len(pieces)
+        for c in range(VALUES):
+            for a in range(TOKEN_TILES):
+                project(c, a)
+                head_squares(c, a)
+                head_rstd(c, a)
+                step = c * TOKEN_TILES + a - key_steps_from
+                if 0 <= step < len(pieces) - 1:
+                    regroup_weights(on_vector, KEYS, *pieces[step])
+                if step == len(pieces) - 1:
+                    quantise_weights(KEYS)
+                if c == KEYS and a == 0:
+                    quantise_weights(VALUES)
+                rotation_products(c, a)
+                add_products(c, a)
+                if c < KEYS:
+                    store(c, a)
+            if c == KEYS - 1:
+                for g, piece in pieces:
+                    regroup_weights(on_scalar, VALUES, g, piece)
+
+        for a in range(TOKEN_TILES):
+            project(VALUES, a)
+            copy_values(a)
+            store(VALUES, a)
+            store(KEYS, a)

@@ -49,10 +49,10 @@ def tile_qwen3block_pa_kernel(tc, x, ln_w, qkv_w, q_norm_w, k_norm_w, out_0, out
         const = ctx.enter_context(tc.tile_pool(name="const", bufs=1))
         keep = ctx.enter_context(tc.tile_pool(name="keep", bufs=1))
         unread = ctx.enter_context(tc.tile_pool(name="unread", bufs=2))
-        grouped_w = ctx.enter_context(tc.tile_pool(name="grouped_w", bufs=2))
+        grouped_w = ctx.enter_context(tc.tile_pool(name="grouped_w", bufs=4))
         stats = ctx.enter_context(tc.tile_pool(name="stats", bufs=8))
         products_pool = ctx.enter_context(tc.tile_pool(name="products_pool", bufs=4))
-        results = ctx.enter_context(tc.tile_pool(name="results", bufs=8))
+        results = ctx.enter_context(tc.tile_pool(name="results", bufs=16))
         psum = ctx.enter_context(tc.psum_pool(name="psum", bufs=8))
         ctx.enter_context(tc.manual_schedule())
 
@@ -61,17 +61,13 @@ def tile_qwen3block_pa_kernel(tc, x, ln_w, qkv_w, q_norm_w, k_norm_w, out_0, out
         identity = const.tile([P, P], BF16)
         eps_col = const.tile([P, 1], F32)
         table_loads = const.tile([P, 2], F32)
-        position_int = const.tile([P, SEQ_TILES], I32)
-        position = const.tile([P, SEQ_TILES], F32)
+        position = const.tile([P, SEQ_TILES], I32)
+        position_turns = const.tile([P, SEQ_TILES], F32)
         inv_freq = const.tile([P, PAIRS], F32)
-        angle = const.tile([P, SEQ_TILES, PAIRS], F32)
-        turns_int = const.tile([P, SEQ_TILES, PAIRS], I32)
-        turns = const.tile([P, SEQ_TILES, PAIRS], F32)
-        partly_reduced = const.tile([P, SEQ_TILES, PAIRS], F32)
-        reduced = const.tile([P, SEQ_TILES, PAIRS], F32)
-        sines_uv = const.tile([P, 2, SEQ_TILES, PAIRS], F32)
-        sines_squared = const.tile([P, 2, SEQ_TILES, PAIRS], F32)
-        minus_two_cos = const.tile([P, SEQ_TILES, PAIRS], F32)
+        turns = const.tile([P, 2, SEQ_TILES, PAIRS], F32)
+        whole_turns = const.tile([P, 2, SEQ_TILES, PAIRS], I32)
+        part_turns = const.tile([P, 2, SEQ_TILES, PAIRS], F32)
+        sincos = const.tile([P, 2, SEQ_TILES, PAIRS], F32)
         rotation = const.tile([P, SEQ_TILES, 2, PAIRS, 2], F32)
         head_gain = const.tile([P, 2, HEAD], F32)
         rope_table = const.tile([P, 2, SEQ_TILES * 2, HEAD], F32)
@@ -97,16 +93,16 @@ def tile_qwen3block_pa_kernel(tc, x, ln_w, qkv_w, q_norm_w, k_norm_w, out_0, out
 
         def constants():
             nc.gpsimd.memset(eps_col[:], EPS)
-            nc.gpsimd.iota(position_int[:], pattern=[[P, SEQ_TILES]], base=0, channel_multiplier=1)
+            nc.gpsimd.iota(position[:], pattern=[[P, SEQ_TILES]], base=0, channel_multiplier=1)
+            nc.gpsimd.memset(gain_rows[:].bitcast(I32), 0)
             nc.gpsimd.memset(ones[:], 1.0)
             make_identity(nc, identity[:])
             nc.scalar.activation(out=table_loads[:, 0:1], in_=eps_col[:], func=ACT.Sin)
 
-        def zero_gain_rows():
-            nc.vector.memset(gain_rows[:].bitcast(I32), 0)
-
         def angles():
-            nc.vector.tensor_copy(out=position[:], in_=position_int[:])
+            nc.vector.tensor_scalar(
+                out=position_turns[:], in0=position[:], scalar1=1.0 / (2.0 * math.pi), scalar2=None, op0=ALU.mult
+            )
             ratio = ROPE_BASE ** (-1.0 / PAIRS)
             nc.vector.memset(inv_freq[:], 1.0)
             for b in range(PAIR_BITS):
@@ -114,54 +110,35 @@ def tile_qwen3block_pa_kernel(tc, x, ln_w, qkv_w, q_norm_w, k_norm_w, out_0, out
                 nc.vector.tensor_scalar(
                     out=bit_set, in0=bit_set, scalar1=ratio ** (2**b), scalar2=None, op0=ALU.mult
                 )
-            for s in range(SEQ_TILES):
-                nc.vector.tensor_scalar(
-                    out=angle[:, s, :],
-                    in0=inv_freq[:],
-                    scalar1=position[:, s : s + 1],
-                    scalar2=-math.pi / 2.0,
-                    op0=ALU.mult,
-                    op1=ALU.add,
-                )
-            nc.vector.tensor_scalar(
-                out=turns_int[:], in0=angle[:], scalar1=1.0 / (2.0 * math.pi), scalar2=0.25, op0=ALU.mult, op1=ALU.add
-            )
-            nc.vector.tensor_copy(out=turns[:], in_=turns_int[:])
-            two_pi_high = 6.28125
-            two_pi_low = 2.0 * math.pi - two_pi_high
-            nc.vector.scalar_tensor_tensor(
-                out=partly_reduced[:], in0=turns[:], scalar=-two_pi_high, in1=angle[:], op0=ALU.mult, op1=ALU.add
-            )
-            nc.vector.scalar_tensor_tensor(
-                out=reduced[:], in0=turns[:], scalar=-two_pi_low, in1=partly_reduced[:], op0=ALU.mult, op1=ALU.add
-            )
+            for quarter in range(2):
+                for s in range(SEQ_TILES):
+                    nc.vector.tensor_scalar(
+                        out=turns[:, quarter, s, :],
+                        in0=inv_freq[:],
+                        scalar1=position_turns[:, s : s + 1],
+                        scalar2=0.25 * quarter,
+                        op0=ALU.mult,
+                        op1=ALU.add,
+                    )
+            nc.vector.tensor_copy(out=whole_turns[:], in_=turns[:])
+            nc.vector.tensor_tensor(out=part_turns[:], in0=turns[:], in1=whole_turns[:], op=ALU.subtract)
 
         def sines():
-            nc.scalar.activation(out=sines_uv[:, 0], in_=reduced[:], func=ACT.Sin, scale=0.5)
-            nc.scalar.activation(out=sines_uv[:, 1], in_=reduced[:], func=ACT.Sin, scale=0.25)
+            nc.scalar.activation(out=sincos[:], in_=part_turns[:], func=ACT.Sin, scale=2.0 * math.pi)
+
+        def rotations():
+            for e, m, quarter, sign in ((0, 0, 1, 1.0), (1, 1, 1, 1.0), (0, 1, 0, -1.0), (1, 0, 0, 1.0)):
+                nc.gpsimd.tensor_scalar(
+                    out=rotation[:, :, e, :, m], in0=sincos[:, quarter], scalar1=sign, scalar2=0.0, op0=ALU.mult, op1=ALU.add
+                )
 
         def load_rsqrt_table():
             nc.scalar.activation(
                 out=table_loads[:, 1:2],
-                in_=sines_uv[:, 0, 0, 0:1],
+                in_=sincos[:, 1, 0, 0:1],
                 func=ACT.Abs_reciprocal_sqrt,
                 bias=eps_col[:, 0:1],
                 scale=0.0,
-            )
-
-        def rotations():
-            u = sines_uv[:, 0]
-            nc.gpsimd.tensor_tensor(out=sines_squared[:], in0=sines_uv[:], in1=sines_uv[:], op=ALU.mult)
-            nc.gpsimd.tensor_scalar(
-                out=minus_two_cos[:], in0=sines_squared[:, 1], scalar1=4.0, scalar2=-2.0, op0=ALU.mult, op1=ALU.add
-            )
-            nc.gpsimd.tensor_tensor(out=rotation[:, :, 0, :, 0], in0=u, in1=minus_two_cos[:], op=ALU.mult)
-            nc.gpsimd.tensor_tensor(out=rotation[:, :, 1, :, 1], in0=u, in1=minus_two_cos[:], op=ALU.mult)
-            nc.gpsimd.tensor_scalar(
-                out=rotation[:, :, 0, :, 1], in0=sines_squared[:, 0], scalar1=2.0, scalar2=-1.0, op0=ALU.mult, op1=ALU.add
-            )
-            nc.gpsimd.tensor_scalar(
-                out=rotation[:, :, 1, :, 0], in0=sines_squared[:, 0], scalar1=-2.0, scalar2=1.0, op0=ALU.mult, op1=ALU.add
             )
 
         def load_x(a):
@@ -183,17 +160,17 @@ def tile_qwen3block_pa_kernel(tc, x, ln_w, qkv_w, q_norm_w, k_norm_w, out_0, out
             )
 
         def spread_gains():
+            spread = psum.tile([P, CHUNK], F32, tag="bank", name="head_gain_psum")
+            nc.tensor.matmul(
+                spread[:, 0 : 2 * HEAD], lhsT=ones[:], rhs=gain_rows[:, MODEL : MODEL + 2 * HEAD], start=True, stop=True
+            )
+            head_gain_psum.append(spread)
             for half in range(2):
                 spread = psum.tile([P, CHUNK], F32, tag="bank", name="ln_w_psum%d" % half)
                 nc.tensor.matmul(
                     spread[:], lhsT=ones[:], rhs=gain_rows[:, half * CHUNK : (half + 1) * CHUNK], start=True, stop=True
                 )
                 ln_w_psum.append(spread)
-            spread = psum.tile([P, CHUNK], F32, tag="bank", name="head_gain_psum")
-            nc.tensor.matmul(
-                spread[:, 0 : 2 * HEAD], lhsT=ones[:], rhs=gain_rows[:, MODEL : MODEL + 2 * HEAD], start=True, stop=True
-            )
-            head_gain_psum.append(spread)
 
         def copy_head_gains():
             nc.scalar.copy(out=head_gain[:].rearrange("p w d -> p (w d)"), in_=head_gain_psum[0][:, 0 : 2 * HEAD])
@@ -210,6 +187,18 @@ def tile_qwen3block_pa_kernel(tc, x, ln_w, qkv_w, q_norm_w, k_norm_w, out_0, out
         def x_squares(a):
             squares = unread.tile([P, MODEL], BF16, tag="x_squares")
             nc.scalar.activation(out=squares[:], in_=x_tile[a][:], func=ACT.Square, accum_out=x_sumsq[:, a : a + 1])
+
+        def x_squares_on_vector(a):
+            squares = unread.tile([P, MODEL], BF16, tag="x_squares")
+            nc.vector.scalar_tensor_tensor(
+                out=squares[:],
+                in0=x_tile[a][:],
+                scalar=1.0,
+                in1=x_tile[a][:],
+                op0=ALU.mult,
+                op1=ALU.mult,
+                accum_out=x_sumsq[:, a : a + 1],
+            )
 
         def x_rstd(a):
             nc.scalar.activation(
@@ -254,12 +243,15 @@ def tile_qwen3block_pa_kernel(tc, x, ln_w, qkv_w, q_norm_w, k_norm_w, out_0, out
                 in_=h_grouped[a][:].rearrange("p g t j -> p (g t j)"),
             )
 
-        def regroup_weights(copy, c, g, piece):
+        def grouped_tile(c):
             if c not in w_grouped:
                 w_grouped[c] = grouped_w.tile(
                     [P, PASSES, CHUNK, PACK], BF16, tag="w_grouped", name="w_grouped%d" % c, align_bytes=64
                 )
-            cols = slice(piece * PIECE, (piece + 1) * PIECE)
+
+        def regroup_weights(copy, c, g, first=0, width=CHUNK):
+            grouped_tile(c)
+            cols = slice(first, first + width)
             copy(
                 out=w_grouped[c][:, g, cols, :].rearrange("p (n i) j -> p n j i", i=4),
                 in_=w_planes[(c, g)][:, :, cols].rearrange("p j (n i) -> p n j i", i=4),
@@ -288,9 +280,10 @@ def tile_qwen3block_pa_kernel(tc, x, ln_w, qkv_w, q_norm_w, k_norm_w, out_0, out
                     stop=(g == PASSES - 1),
                 )
 
-        def head_squares(c, a):
-            head_sumsq[(c, a)] = stats.tile([P, HEADS], F32, tag="head_sumsq", name="head_sumsq")
-            for h in range(HEADS):
+        def head_squares(c, a, heads):
+            if (c, a) not in head_sumsq:
+                head_sumsq[(c, a)] = stats.tile([P, HEADS], F32, tag="head_sumsq", name="head_sumsq")
+            for h in heads:
                 squares = unread.tile([P, HEAD], BF16, tag="head_squares")
                 nc.scalar.activation(
                     out=squares[:],
@@ -309,11 +302,14 @@ def tile_qwen3block_pa_kernel(tc, x, ln_w, qkv_w, q_norm_w, k_norm_w, out_0, out
                 scale=1.0 / HEAD,
             )
 
-        def rotation_products(c, a):
+        def rotation_products(c, a, heads):
             gain = chunk_target[c][2]
             first = 2 * (a % SEQ_TILES)
-            pair_products[(c, a)] = products_pool.tile([P, HEADS, 2, HEAD], F32, tag="pair_products", name="pair_products")
-            for h in range(HEADS):
+            if (c, a) not in pair_products:
+                pair_products[(c, a)] = products_pool.tile(
+                    [P, HEADS, 2, HEAD], F32, tag="pair_products", name="pair_products"
+                )
+            for h in heads:
                 nc.vector.scalar_tensor_tensor(
                     out=pair_products[(c, a)][:, h],
                     in0=bank[(c, a)][:, h * HEAD : (h + 1) * HEAD].unsqueeze(1).to_broadcast([P, 2, HEAD]),
@@ -323,13 +319,14 @@ def tile_qwen3block_pa_kernel(tc, x, ln_w, qkv_w, q_norm_w, k_norm_w, out_0, out
                     op1=ALU.mult,
                 )
 
-        def add_products(c, a):
-            result[(c, a)] = results.tile([P, CHUNK], F32, tag="result", name="result")
+        def add_products(engine, c, a, heads):
+            if (c, a) not in result:
+                result[(c, a)] = results.tile([P, CHUNK], F32, tag="result", name="result")
             by_m = pair_products[(c, a)][:].rearrange("p h e (j m) -> p h j e m", m=2)
-            nc.gpsimd.tensor_tensor(
-                out=result[(c, a)][:].rearrange("p (h j e) -> p h j e", h=HEADS, e=2),
-                in0=by_m[:, :, :, :, 0],
-                in1=by_m[:, :, :, :, 1],
+            engine.tensor_tensor(
+                out=result[(c, a)][:].rearrange("p (h j e) -> p h j e", h=HEADS, e=2)[:, heads],
+                in0=by_m[:, heads, :, :, 0],
+                in1=by_m[:, heads, :, :, 1],
                 op=ALU.add,
             )
 
@@ -337,35 +334,36 @@ def tile_qwen3block_pa_kernel(tc, x, ln_w, qkv_w, q_norm_w, k_norm_w, out_0, out
             result[(VALUES, a)] = results.tile([P, CHUNK], F32, tag="result", name="result")
             nc.scalar.copy(out=result[(VALUES, a)][:], in_=bank[(VALUES, a)][:])
 
-        def store(c, a):
+        def store(c, a, first_head=0, heads=HEADS):
             target, first_col, gain = chunk_target[c]
-            nc.sync.dma_start(out=target[a * P : (a + 1) * P, first_col : first_col + CHUNK], in_=result[(c, a)][:])
+            cols = slice(first_head * HEAD, (first_head + heads) * HEAD)
+            nc.sync.dma_start(
+                out=target[a * P : (a + 1) * P, first_col + cols.start : first_col + cols.stop],
+                in_=result[(c, a)][:, cols],
+            )
 
         on_vector = nc.vector.tensor_copy
         on_scalar = nc.scalar.copy
-        pieces = [(g, piece) for g in range(PASSES) for piece in range(PIECES)]
 
         constants()
-        zero_gain_rows()
         load_x(0)
-        load_gains()
         load_weights(0, 0)
-        load_x(1)
+        load_gains()
         load_weights(0, 1)
+        load_x(1)
         load_x(2)
         load_x(3)
         for c in range(1, CHUNKS):
             for g in range(PASSES):
                 load_weights(c, g)
         angles()
-
         x_squares(0)
         sines()
         load_rsqrt_table()
         rotations()
         spread_gains()
-        for g, piece in pieces:
-            regroup_weights(on_vector, 0, g, piece)
+        for g in range(PASSES):
+            regroup_weights(on_vector, 0, g)
         x_rstd(0)
         for a in range(1, TOKEN_TILES):
             x_squares(a)
@@ -382,41 +380,51 @@ def tile_qwen3block_pa_kernel(tc, x, ln_w, qkv_w, q_norm_w, k_norm_w, out_0, out
         transpose_h(last)
         group_h(1)
         quantise_h(1)
-        regroup_weights(on_vector, 1, *pieces[0])
+        regroup_weights(on_vector, 1, 0)
         group_h(2)
         quantise_h(2)
         copy_head_gains()
         rope_tables()
-        regroup_weights(on_scalar, KEYS, *pieces[-1])
-        for g, piece in pieces[1:]:
-            regroup_weights(on_vector, 1, g, piece)
+        regroup_weights(on_scalar, 1, 1, PIECE, PIECE)
+        regroup_weights(on_vector, 1, 1, 0, PIECE)
         quantise_weights(1)
         group_h(last)
         quantise_h(last)
 
-        key_steps_from = KEYS * TOKEN_TILES - 2 - len(pieces)
-        for c in range(VALUES):
-            for a in range(TOKEN_TILES):
-                project(c, a)
-                head_squares(c, a)
-                head_rstd(c, a)
-                step = c * TOKEN_TILES + a - key_steps_from
-                if 0 <= step < len(pieces) - 1:
-                    regroup_weights(on_vector, KEYS, *pieces[step])
-                if step == len(pieces) - 1:
-                    quantise_weights(KEYS)
-                if c == KEYS and a == 0:
-                    quantise_weights(VALUES)
-                rotation_products(c, a)
-                add_products(c, a)
+        banks = [(c, a) for c in range(VALUES) for a in range(TOKEN_TILES)]
+        project(*banks[0])
+        head_squares(*banks[0], range(HEADS))
+        for i, (c, a) in enumerate(banks):
+            if i + 1 < len(banks):
+                project(*banks[i + 1])
+                head_squares(*banks[i + 1], range(1))
+            head_rstd(c, a)
+            if i + 1 < len(banks):
+                head_squares(*banks[i + 1], range(1, HEADS))
+            if i == 3:
+                regroup_weights(on_vector, KEYS, 0)
+            if i == 5:
+                quantise_weights(KEYS)
+            if i == 8:
+                quantise_weights(VALUES)
+            rotation_products(c, a, range(HEADS))
+            if i + 1 < len(banks):
+                add_products(nc.gpsimd, c, a, slice(0, HEADS))
                 if c < KEYS:
                     store(c, a)
-            if c == KEYS - 1:
-                for g, piece in pieces:
-                    regroup_weights(on_scalar, VALUES, g, piece)
+            else:
+                for first in (0, 2):
+                    add_products(nc.vector, c, a, slice(first, first + 2))
+            if i in (1, 2):
+                regroup_weights(on_scalar, KEYS, 1, (1, 2).index(i) * PIECE, PIECE)
+            if i in (5, 7):
+                regroup_weights(on_scalar, VALUES, (5, 7).index(i))
 
         for a in range(TOKEN_TILES):
             project(VALUES, a)
             copy_values(a)
             store(VALUES, a)
-            store(KEYS, a)
+            if a < last:
+                store(KEYS, a)
+        for first in (0, 2):
+            store(KEYS, last, first, 2)

@@ -20,7 +20,6 @@ MODEL = 1024
 FUSED = 2048
 HEAD = 128
 PAIRS = HEAD // 2
-PAIR_BITS = 6
 TOKEN_TILES = TOKENS // P
 CHUNK = 512
 CHUNKS = FUSED // CHUNK
@@ -104,12 +103,16 @@ def tile_qwen3block_pa_kernel(tc, x, ln_w, qkv_w, q_norm_w, k_norm_w, out_0, out
                 out=position_turns[:], in0=position[:], scalar1=1.0 / (2.0 * math.pi), scalar2=None, op0=ALU.mult
             )
             ratio = ROPE_BASE ** (-1.0 / PAIRS)
-            nc.vector.memset(inv_freq[:], 1.0)
-            for b in range(PAIR_BITS):
-                bit_set = inv_freq[:].rearrange("p (q t r) -> p q t r", t=2, r=2**b)[:, :, 1, :]
-                nc.vector.tensor_scalar(
-                    out=bit_set, in0=bit_set, scalar1=ratio ** (2**b), scalar2=None, op0=ALU.mult
-                )
+            nc.vector.memset(inv_freq[:, 0:1], 1.0)
+            for done in (1, 4, 16):
+                for run in (1, 2, 3):
+                    nc.vector.tensor_scalar(
+                        out=inv_freq[:, run * done : (run + 1) * done],
+                        in0=inv_freq[:, 0:done],
+                        scalar1=ratio ** (run * done),
+                        scalar2=None,
+                        op0=ALU.mult,
+                    )
             for quarter in range(2):
                 for s in range(SEQ_TILES):
                     nc.vector.tensor_scalar(
@@ -150,13 +153,13 @@ def tile_qwen3block_pa_kernel(tc, x, ln_w, qkv_w, q_norm_w, k_norm_w, out_0, out
             nc.sync.dma_start(out=gain_rows[0:1, MODEL : MODEL + HEAD], in_=q_norm_w.unsqueeze(0))
             nc.sync.dma_start(out=gain_rows[0:1, MODEL + HEAD : MODEL + 2 * HEAD], in_=k_norm_w.unsqueeze(0))
 
-        def load_weights(c, g):
-            w_planes[(c, g)] = keep.tile([P, PACK, CHUNK], BF16, name="w_planes%d%d" % (c, g))
+        def load_weights(c, g, first=0, width=CHUNK):
+            if (c, g) not in w_planes:
+                w_planes[(c, g)] = keep.tile([P, PACK, CHUNK], BF16, name="w_planes%d%d" % (c, g))
+            cols = slice(c * CHUNK + first, c * CHUNK + first + width)
             nc.sync.dma_start(
-                out=w_planes[(c, g)][:],
-                in_=qkv_w[g * PASS_ROWS : (g + 1) * PASS_ROWS, c * CHUNK : (c + 1) * CHUNK].rearrange(
-                    "(j p) n -> p j n", p=P
-                ),
+                out=w_planes[(c, g)][:, :, first : first + width],
+                in_=qkv_w[g * PASS_ROWS : (g + 1) * PASS_ROWS, cols].rearrange("(j p) n -> p j n", p=P),
             )
 
         def spread_gains():
@@ -257,6 +260,18 @@ def tile_qwen3block_pa_kernel(tc, x, ln_w, qkv_w, q_norm_w, k_norm_w, out_0, out
                 in_=w_planes[(c, g)][:, :, cols].rearrange("p j (n i) -> p n j i", i=4),
             )
 
+        def regroup_on_gpsimd(c, g, first=0, width=CHUNK):
+            grouped_tile(c)
+            cols = slice(first, first + width)
+            nc.gpsimd.tensor_scalar(
+                out=w_grouped[c][:, g, cols, :],
+                in0=w_planes[(c, g)][:, :, cols].rearrange("p j n -> p n j"),
+                scalar1=1.0,
+                scalar2=0.0,
+                op0=ALU.mult,
+                op1=ALU.add,
+            )
+
         def quantise_weights(c):
             w_codes[c] = keep.tile([P, PASSES, CHUNK], U32, name="w_codes%d" % c, align_bytes=64)
             w_scales[c] = keep.tile([P, PASSES, CHUNK], U8, name="w_scales%d" % c, align_bytes=64)
@@ -348,16 +363,16 @@ def tile_qwen3block_pa_kernel(tc, x, ln_w, qkv_w, q_norm_w, k_norm_w, out_0, out
         constants()
         load_x(0)
         load_weights(0, 0)
+        load_x(1)
         load_gains()
         load_weights(0, 1)
-        load_x(1)
         load_x(2)
         load_x(3)
         for c in range(1, CHUNKS):
             for g in range(PASSES):
                 load_weights(c, g)
         angles()
-        x_squares(0)
+        x_squares_on_vector(0)
         sines()
         load_rsqrt_table()
         rotations()
@@ -365,9 +380,15 @@ def tile_qwen3block_pa_kernel(tc, x, ln_w, qkv_w, q_norm_w, k_norm_w, out_0, out
         for g in range(PASSES):
             regroup_weights(on_vector, 0, g)
         x_rstd(0)
-        for a in range(1, TOKEN_TILES):
-            x_squares(a)
-            x_rstd(a)
+        x_squares(1)
+        copy_head_gains()
+        x_rstd(1)
+        x_squares(2)
+        x_rstd(2)
+        x_squares(3)
+        x_rstd(3)
+        rope_tables()
+
 
         last = TOKEN_TILES - 1
         for a in range(last):
@@ -383,13 +404,13 @@ def tile_qwen3block_pa_kernel(tc, x, ln_w, qkv_w, q_norm_w, k_norm_w, out_0, out
         regroup_weights(on_vector, 1, 0)
         group_h(2)
         quantise_h(2)
-        copy_head_gains()
-        rope_tables()
+
         regroup_weights(on_scalar, 1, 1, PIECE, PIECE)
         regroup_weights(on_vector, 1, 1, 0, PIECE)
         quantise_weights(1)
         group_h(last)
         quantise_h(last)
+
 
         banks = [(c, a) for c in range(VALUES) for a in range(TOKEN_TILES)]
         project(*banks[0])
@@ -405,20 +426,23 @@ def tile_qwen3block_pa_kernel(tc, x, ln_w, qkv_w, q_norm_w, k_norm_w, out_0, out
                 regroup_weights(on_vector, KEYS, 0)
             if i == 5:
                 quantise_weights(KEYS)
-            if i == 8:
+            if i == 6:
+                regroup_weights(on_vector, VALUES, 0)
+            if i == 7:
                 quantise_weights(VALUES)
-            rotation_products(c, a, range(HEADS))
             if i + 1 < len(banks):
+                rotation_products(c, a, range(HEADS))
                 add_products(nc.gpsimd, c, a, slice(0, HEADS))
                 if c < KEYS:
                     store(c, a)
             else:
+                rotation_products(c, a, range(HEADS))
                 for first in (0, 2):
                     add_products(nc.vector, c, a, slice(first, first + 2))
             if i in (1, 2):
-                regroup_weights(on_scalar, KEYS, 1, (1, 2).index(i) * PIECE, PIECE)
-            if i in (5, 7):
-                regroup_weights(on_scalar, VALUES, (5, 7).index(i))
+                regroup_weights(on_scalar, KEYS, 1, (i - 1) * PIECE, PIECE)
+            if i == 6:
+                regroup_weights(on_scalar, VALUES, 1)
 
         for a in range(TOKEN_TILES):
             project(VALUES, a)

@@ -168,12 +168,11 @@ def tile_qwen3block_pa_kernel(tc, x, ln_w, qkv_w, q_norm_w, k_norm_w, out_0, out
                 spread[:, 0 : 2 * HEAD], lhsT=ones[:], rhs=gain_rows[:, MODEL : MODEL + 2 * HEAD], start=True, stop=True
             )
             head_gain_psum.append(spread)
+            spread = psum.tile([P, MODEL], BF16, tag="bank", name="ln_w_psum")
             for half in range(2):
-                spread = psum.tile([P, CHUNK], F32, tag="bank", name="ln_w_psum%d" % half)
-                nc.tensor.matmul(
-                    spread[:], lhsT=ones[:], rhs=gain_rows[:, half * CHUNK : (half + 1) * CHUNK], start=True, stop=True
-                )
-                ln_w_psum.append(spread)
+                cols = slice(half * CHUNK, (half + 1) * CHUNK)
+                nc.tensor.matmul(spread[:, cols], lhsT=ones[:], rhs=gain_rows[:, cols], start=True, stop=True)
+            ln_w_psum.append(spread)
 
         def copy_head_gains():
             nc.scalar.copy(out=head_gain[:].rearrange("p w d -> p (w d)"), in_=head_gain_psum[0][:, 0 : 2 * HEAD])
@@ -214,16 +213,14 @@ def tile_qwen3block_pa_kernel(tc, x, ln_w, qkv_w, q_norm_w, k_norm_w, out_0, out
 
         def normalise(a):
             h_tile[a] = keep.tile([P, MODEL], BF16, name="h_tile%d" % a)
-            for half in range(2):
-                cols = slice(half * CHUNK, (half + 1) * CHUNK)
-                nc.vector.scalar_tensor_tensor(
-                    out=h_tile[a][:, cols],
-                    in0=x_tile[a][:, cols],
-                    scalar=x_rstd_cols[:, a : a + 1],
-                    in1=ln_w_psum[half][:],
-                    op0=ALU.mult,
-                    op1=ALU.mult,
-                )
+            nc.vector.scalar_tensor_tensor(
+                out=h_tile[a][:],
+                in0=x_tile[a][:],
+                scalar=x_rstd_cols[:, a : a + 1],
+                in1=ln_w_psum[0][:],
+                op0=ALU.mult,
+                op1=ALU.mult,
+            )
 
         def transpose_h(a):
             h_transposed[a] = psum.tile([P, MODEL], BF16, tag="bank", name="h_transposed%d" % a)
@@ -389,28 +386,25 @@ def tile_qwen3block_pa_kernel(tc, x, ln_w, qkv_w, q_norm_w, k_norm_w, out_0, out
         x_rstd(3)
         rope_tables()
 
-
-        last = TOKEN_TILES - 1
-        for a in range(last):
+        for a in range(TOKEN_TILES):
             normalise(a)
             transpose_h(a)
+            group_h(a)
+        regroup_weights(on_scalar, 1, 1, PIECE, PIECE)
         quantise_weights(0)
-        group_h(0)
         quantise_h(0)
-        normalise(last)
-        transpose_h(last)
-        group_h(1)
         quantise_h(1)
         regroup_weights(on_vector, 1, 0)
-        group_h(2)
         quantise_h(2)
-
-        regroup_weights(on_scalar, 1, 1, PIECE, PIECE)
         regroup_weights(on_vector, 1, 1, 0, PIECE)
+        quantise_h(3)
+        regroup_weights(on_scalar, KEYS, 1)
+        regroup_weights(on_vector, KEYS, 0)
         quantise_weights(1)
-        group_h(last)
-        quantise_h(last)
-
+        regroup_weights(on_scalar, VALUES, 1)
+        regroup_weights(on_vector, VALUES, 0)
+        quantise_weights(KEYS)
+        quantise_weights(VALUES)
 
         banks = [(c, a) for c in range(VALUES) for a in range(TOKEN_TILES)]
         project(*banks[0])
@@ -422,33 +416,15 @@ def tile_qwen3block_pa_kernel(tc, x, ln_w, qkv_w, q_norm_w, k_norm_w, out_0, out
             head_rstd(c, a)
             if i + 1 < len(banks):
                 head_squares(*banks[i + 1], range(1, HEADS))
-            if i == 3:
-                regroup_weights(on_vector, KEYS, 0)
-            if i == 5:
-                quantise_weights(KEYS)
-            if i == 6:
-                regroup_weights(on_vector, VALUES, 0)
-            if i == 7:
-                quantise_weights(VALUES)
+            rotation_products(c, a, range(HEADS))
             if i + 1 < len(banks):
-                rotation_products(c, a, range(HEADS))
                 add_products(nc.gpsimd, c, a, slice(0, HEADS))
-                if c < KEYS:
-                    store(c, a)
+                store(c, a)
             else:
-                rotation_products(c, a, range(HEADS))
                 for first in (0, 2):
                     add_products(nc.vector, c, a, slice(first, first + 2))
-            if i in (1, 2):
-                regroup_weights(on_scalar, KEYS, 1, (i - 1) * PIECE, PIECE)
-            if i == 6:
-                regroup_weights(on_scalar, VALUES, 1)
-
-        for a in range(TOKEN_TILES):
-            project(VALUES, a)
-            copy_values(a)
-            store(VALUES, a)
-            if a < last:
-                store(KEYS, a)
-        for first in (0, 2):
-            store(KEYS, last, first, 2)
+                    store(c, a, first, 2)
+            if 5 <= i < 9:
+                project(VALUES, i - 5)
+                copy_values(i - 5)
+                store(VALUES, i - 5)

import math
from contextlib import ExitStack

import concourse.mybir as mybir
from concourse.masks import make_identity

F32 = mybir.dt.float32
BF16 = mybir.dt.bfloat16
I32 = mybir.dt.int32
U32 = mybir.dt.uint32
U8 = mybir.dt.uint8
FP8X4 = mybir.dt.float8_e4m3fn_x4
ALU = mybir.AluOpType
ACT = mybir.ActivationFunctionType

P = 128
TOKENS = 512
SEQ_TILES = 2
MODEL = 1024
FUSED = 2048
HEAD = 128
PAIRS = HEAD // 2
TOKEN_TILES = TOKENS // P
CHUNK = 512
CHUNKS = FUSED // CHUNK
HEADS = CHUNK // HEAD
PACK = 4
PASS_ROWS = P * PACK
PASSES = MODEL // PASS_ROWS
PIECE = 256
PIECES = CHUNK // PIECE
EPS = 1e-6
ROPE_BASE = 1000000.0
KEYS = 2
VALUES = 3
FLOPS = 2 * TOKENS * MODEL * FUSED


def tile_qwen3block_pa_kernel(tc, x, ln_w, qkv_w, q_norm_w, k_norm_w, out_0, out_1, out_2):
    nc = tc.nc
    x_rows = x.flatten_outer_dims()
    queries = out_0.rearrange("b s h d -> (b s) (h d)")
    keys = out_1.rearrange("b s h d -> (b s) (h d)")
    values_out = out_2.rearrange("b s h d -> (b s) (h d)")
    chunk_target = [(queries, 0, 0), (queries, CHUNK, 0), (keys, 0, 1), (values_out, 0, None)]

    with ExitStack() as ctx:
        const = ctx.enter_context(tc.tile_pool(name="const", bufs=1))
        keep = ctx.enter_context(tc.tile_pool(name="keep", bufs=1))
        unread = ctx.enter_context(tc.tile_pool(name="unread", bufs=2))
        grouped_w = ctx.enter_context(tc.tile_pool(name="grouped_w", bufs=4))
        stats = ctx.enter_context(tc.tile_pool(name="stats", bufs=8))
        products_pool = ctx.enter_context(tc.tile_pool(name="products_pool", bufs=4))
        results = ctx.enter_context(tc.tile_pool(name="results", bufs=16))
        psum = ctx.enter_context(tc.psum_pool(name="psum", bufs=8))
        ctx.enter_context(tc.manual_schedule())

        gain_rows = const.tile([P, MODEL + 2 * HEAD], BF16)
        ones = const.tile([P, P], BF16)
        identity = const.tile([P, P], BF16)
        eps_col = const.tile([P, 1], F32)
        table_loads = const.tile([P, 2], F32)
        position = const.tile([P, SEQ_TILES], I32)
        position_turns = const.tile([P, SEQ_TILES], F32)
        inv_freq = const.tile([P, PAIRS], F32)
        turns = const.tile([P, 2, SEQ_TILES, PAIRS], F32)
        whole_turns = const.tile([P, 2, SEQ_TILES, PAIRS], I32)
        part_turns = const.tile([P, 2, SEQ_TILES, PAIRS], F32)
        sincos = const.tile([P, 2, SEQ_TILES, PAIRS], F32)
        rotation = const.tile([P, SEQ_TILES, 2, PAIRS, 2], F32)
        head_gain = const.tile([P, 2, HEAD], F32)
        rope_table = const.tile([P, 2, SEQ_TILES * 2, HEAD], F32)
        x_sumsq = const.tile([P, TOKEN_TILES], F32)
        x_rstd_cols = const.tile([P, TOKEN_TILES], F32)
        x_tile = {}
        w_planes = {}
        ln_w_psum = []
        head_gain_psum = []
        h_tile = {}
        h_transposed = {}
        h_grouped = {}
        h_codes = {}
        h_scales = {}
        w_grouped = {}
        w_codes = {}
        w_scales = {}
        bank = {}
        head_sumsq = {}
        head_rstd_cols = {}
        pair_products = {}
        result = {}

        def constants():
            nc.gpsimd.memset(eps_col[:], EPS)
            nc.gpsimd.iota(position[:], pattern=[[P, SEQ_TILES]], base=0, channel_multiplier=1)
            nc.gpsimd.memset(gain_rows[:].bitcast(I32), 0)
            nc.gpsimd.memset(ones[:], 1.0)
            make_identity(nc, identity[:])
            nc.scalar.activation(out=table_loads[:, 0:1], in_=eps_col[:], func=ACT.Sin)

        def angles():
            nc.vector.tensor_scalar(
                out=position_turns[:], in0=position[:], scalar1=1.0 / (2.0 * math.pi), scalar2=None, op0=ALU.mult
            )
            ratio = ROPE_BASE ** (-1.0 / PAIRS)
            nc.vector.memset(inv_freq[:, 0:1], 1.0)
            for done in (1, 4, 16):
                for run in (1, 2, 3):
                    nc.vector.tensor_scalar(
                        out=inv_freq[:, run * done : (run + 1) * done],
                        in0=inv_freq[:, 0:done],
                        scalar1=ratio ** (run * done),
                        scalar2=None,
                        op0=ALU.mult,
                    )
            for quarter in range(2):
                for s in range(SEQ_TILES):
                    nc.vector.tensor_scalar(
                        out=turns[:, quarter, s, :],
                        in0=inv_freq[:],
                        scalar1=position_turns[:, s : s + 1],
                        scalar2=0.25 * quarter,
                        op0=ALU.mult,
                        op1=ALU.add,
                    )
            nc.vector.tensor_copy(out=whole_turns[:], in_=turns[:])
            nc.vector.tensor_tensor(out=part_turns[:], in0=turns[:], in1=whole_turns[:], op=ALU.subtract)

        def sines():
            nc.scalar.activation(out=sincos[:], in_=part_turns[:], func=ACT.Sin, scale=2.0 * math.pi)

        def rotations():
            for e, m, quarter, sign in ((0, 0, 1, 1.0), (1, 1, 1, 1.0), (0, 1, 0, -1.0), (1, 0, 0, 1.0)):
                nc.gpsimd.tensor_scalar(
                    out=rotation[:, :, e, :, m], in0=sincos[:, quarter], scalar1=sign, scalar2=0.0, op0=ALU.mult, op1=ALU.add
                )

        def load_rsqrt_table():
            nc.scalar.activation(
                out=table_loads[:, 1:2],
                in_=sincos[:, 1, 0, 0:1],
                func=ACT.Abs_reciprocal_sqrt,
                bias=eps_col[:, 0:1],
                scale=0.0,
            )

        def load_x(a):
            x_tile[a] = keep.tile([P, MODEL], BF16, name="x_tile%d" % a)
            nc.sync.dma_start(out=x_tile[a][:], in_=x_rows[a * P : (a + 1) * P, :])

        def load_gains():
            nc.sync.dma_start(out=gain_rows[0:1, 0:MODEL], in_=ln_w.unsqueeze(0))
            nc.sync.dma_start(out=gain_rows[0:1, MODEL : MODEL + HEAD], in_=q_norm_w.unsqueeze(0))
            nc.sync.dma_start(out=gain_rows[0:1, MODEL + HEAD : MODEL + 2 * HEAD], in_=k_norm_w.unsqueeze(0))

        def load_weights(c, g, first=0, width=CHUNK):
            if (c, g) not in w_planes:
                w_planes[(c, g)] = keep.tile([P, PACK, CHUNK], BF16, name="w_planes%d%d" % (c, g))
            cols = slice(c * CHUNK + first, c * CHUNK + first + width)
            nc.sync.dma_start(
                out=w_planes[(c, g)][:, :, first : first + width],
                in_=qkv_w[g * PASS_ROWS : (g + 1) * PASS_ROWS, cols].rearrange("(j p) n -> p j n", p=P),
            )

        def spread_gains():
            spread = psum.tile([P, CHUNK], F32, tag="bank", name="head_gain_psum")
            nc.tensor.matmul(
                spread[:, 0 : 2 * HEAD], lhsT=ones[:], rhs=gain_rows[:, MODEL : MODEL + 2 * HEAD], start=True, stop=True
            )
            head_gain_psum.append(spread)
            spread = psum.tile([P, MODEL], BF16, tag="bank", name="ln_w_psum")
            for half in range(2):
                cols = slice(half * CHUNK, (half + 1) * CHUNK)
                nc.tensor.matmul(spread[:, cols], lhsT=ones[:], rhs=gain_rows[:, cols], start=True, stop=True)
            ln_w_psum.append(spread)

        def copy_head_gains():
            nc.scalar.copy(out=head_gain[:].rearrange("p w d -> p (w d)"), in_=head_gain_psum[0][:, 0 : 2 * HEAD])

        def rope_tables():
            for w in range(2):
                nc.gpsimd.tensor_tensor(
                    out=rope_table[:, w],
                    in0=rotation[:].rearrange("p s e j m -> p (s e) (j m)"),
                    in1=head_gain[:, w, :].unsqueeze(1).to_broadcast([P, SEQ_TILES * 2, HEAD]),
                    op=ALU.mult,
                )

        def x_squares(a):
            squares = unread.tile([P, MODEL], BF16, tag="x_squares")
            nc.scalar.activation(out=squares[:], in_=x_tile[a][:], func=ACT.Square, accum_out=x_sumsq[:, a : a + 1])

        def x_squares_on_vector(a):
            squares = unread.tile([P, MODEL], BF16, tag="x_squares")
            nc.vector.scalar_tensor_tensor(
                out=squares[:],
                in0=x_tile[a][:],
                scalar=1.0,
                in1=x_tile[a][:],
                op0=ALU.mult,
                op1=ALU.mult,
                accum_out=x_sumsq[:, a : a + 1],
            )

        def x_rstd(a):
            nc.scalar.activation(
                out=x_rstd_cols[:, a : a + 1],
                in_=x_sumsq[:, a : a + 1],
                func=ACT.Abs_reciprocal_sqrt,
                bias=eps_col[:, 0:1],
                scale=1.0 / MODEL,
            )

        def normalise(a):
            h_tile[a] = keep.tile([P, MODEL], BF16, name="h_tile%d" % a)
            nc.vector.scalar_tensor_tensor(
                out=h_tile[a][:],
                in0=x_tile[a][:],
                scalar=x_rstd_cols[:, a : a + 1],
                in1=ln_w_psum[0][:],
                op0=ALU.mult,
                op1=ALU.mult,
            )

        def transpose_h(a):
            h_transposed[a] = psum.tile([P, MODEL], BF16, tag="bank", name="h_transposed%d" % a)
            for block in range(MODEL // P):
                cols = slice(block * P, (block + 1) * P)
                nc.tensor.transpose(h_transposed[a][:, cols], h_tile[a][:, cols], identity[:])

        def group_h(a):
            h_grouped[a] = keep.tile([P, PASSES, P, PACK], BF16, name="h_grouped%d" % a, align_bytes=64)
            nc.scalar.copy(
                out=h_grouped[a][:], in_=h_transposed[a][:].rearrange("p (g j t) -> p g t j", g=PASSES, j=PACK)
            )

        def quantise_h(a):
            h_codes[a] = keep.tile([P, PASSES * P], U32, name="h_codes%d" % a, align_bytes=64)
            h_scales[a] = keep.tile([P, PASSES * P], U8, name="h_scales%d" % a, align_bytes=64)
            nc.vector.quantize_mx(
                out=h_codes[a][:].bitcast(FP8X4),
                scales=h_scales[a][:],
                in_=h_grouped[a][:].rearrange("p g t j -> p (g t j)"),
            )

        def grouped_tile(c):
            if c not in w_grouped:
                w_grouped[c] = grouped_w.tile(
                    [P, PASSES, CHUNK, PACK], BF16, tag="w_grouped", name="w_grouped%d" % c, align_bytes=64
                )

        def regroup_weights(copy, c, g, first=0, width=CHUNK):
            grouped_tile(c)
            cols = slice(first, first + width)
            copy(
                out=w_grouped[c][:, g, cols, :].rearrange("p (n i) j -> p n j i", i=4),
                in_=w_planes[(c, g)][:, :, cols].rearrange("p j (n i) -> p n j i", i=4),
            )

        def regroup_on_gpsimd(c, g, first=0, width=CHUNK):
            grouped_tile(c)
            cols = slice(first, first + width)
            nc.gpsimd.tensor_scalar(
                out=w_grouped[c][:, g, cols, :],
                in0=w_planes[(c, g)][:, :, cols].rearrange("p j n -> p n j"),
                scalar1=1.0,
                scalar2=0.0,
                op0=ALU.mult,
                op1=ALU.add,
            )

        def quantise_weights(c):
            w_codes[c] = keep.tile([P, PASSES, CHUNK], U32, name="w_codes%d" % c, align_bytes=64)
            w_scales[c] = keep.tile([P, PASSES, CHUNK], U8, name="w_scales%d" % c, align_bytes=64)
            nc.vector.quantize_mx(
                out=w_codes[c][:].rearrange("p g n -> p (g n)").bitcast(FP8X4),
                scales=w_scales[c][:].rearrange("p g n -> p (g n)"),
                in_=w_grouped[c][:].rearrange("p g n j -> p (g n j)"),
            )

        def project(c, a):
            bank[(c, a)] = psum.tile([P, CHUNK], F32, tag="bank", name="bank")
            for g in range(PASSES):
                tokens = slice(g * P, (g + 1) * P)
                nc.tensor.matmul_mx(
                    out=bank[(c, a)][:],
                    lhsT=h_codes[a][:, tokens].bitcast(FP8X4),
                    lhsT_scale=h_scales[a][:, tokens],
                    rhs=w_codes[c][:, g, :].bitcast(FP8X4),
                    rhs_scale=w_scales[c][:, g, :],
                    start=(g == 0),
                    stop=(g == PASSES - 1),
                )

        def head_squares(c, a, heads):
            if (c, a) not in head_sumsq:
                head_sumsq[(c, a)] = stats.tile([P, HEADS], F32, tag="head_sumsq", name="head_sumsq")
            for h in heads:
                squares = unread.tile([P, HEAD], BF16, tag="head_squares")
                nc.scalar.activation(
                    out=squares[:],
                    in_=bank[(c, a)][:, h * HEAD : (h + 1) * HEAD],
                    func=ACT.Square,
                    accum_out=head_sumsq[(c, a)][:, h : h + 1],
                )

        def head_rstd(c, a):
            head_rstd_cols[(c, a)] = stats.tile([P, HEADS], F32, tag="head_rstd", name="head_rstd")
            nc.scalar.activation(
                out=head_rstd_cols[(c, a)][:],
                in_=head_sumsq[(c, a)][:],
                func=ACT.Abs_reciprocal_sqrt,
                bias=eps_col[:, 0:1],
                scale=1.0 / HEAD,
            )

        def rotation_products(c, a, heads):
            gain = chunk_target[c][2]
            first = 2 * (a % SEQ_TILES)
            if (c, a) not in pair_products:
                pair_products[(c, a)] = products_pool.tile(
                    [P, HEADS, 2, HEAD], F32, tag="pair_products", name="pair_products"
                )
            for h in heads:
                nc.vector.scalar_tensor_tensor(
                    out=pair_products[(c, a)][:, h],
                    in0=bank[(c, a)][:, h * HEAD : (h + 1) * HEAD].unsqueeze(1).to_broadcast([P, 2, HEAD]),
                    scalar=head_rstd_cols[(c, a)][:, h : h + 1],
                    in1=rope_table[:, gain, first : first + 2, :],
                    op0=ALU.mult,
                    op1=ALU.mult,
                )

        def add_products(engine, c, a, heads):
            if (c, a) not in result:
                result[(c, a)] = results.tile([P, CHUNK], F32, tag="result", name="result")
            by_m = pair_products[(c, a)][:].rearrange("p h e (j m) -> p h j e m", m=2)
            engine.tensor_tensor(
                out=result[(c, a)][:].rearrange("p (h j e) -> p h j e", h=HEADS, e=2)[:, heads],
                in0=by_m[:, heads, :, :, 0],
                in1=by_m[:, heads, :, :, 1],
                op=ALU.add,
            )

        def copy_values(a):
            result[(VALUES, a)] = results.tile([P, CHUNK], F32, tag="result", name="result")
            nc.scalar.copy(out=result[(VALUES, a)][:], in_=bank[(VALUES, a)][:])

        def store(c, a, first_head=0, heads=HEADS):
            target, first_col, gain = chunk_target[c]
            cols = slice(first_head * HEAD, (first_head + heads) * HEAD)
            nc.sync.dma_start(
                out=target[a * P : (a + 1) * P, first_col + cols.start : first_col + cols.stop],
                in_=result[(c, a)][:, cols],
            )

        on_vector = nc.vector.tensor_copy
        on_scalar = nc.scalar.copy

        constants()
        load_x(0)
        load_weights(0, 0)
        load_x(1)
        load_gains()
        load_weights(0, 1)
        load_x(2)
        load_x(3)
        for c in range(1, CHUNKS):
            for g in range(PASSES):
                load_weights(c, g)
        angles()
        x_squares_on_vector(0)
        sines()
        load_rsqrt_table()
        rotations()
        spread_gains()
        for g in range(PASSES):
            regroup_weights(on_vector, 0, g)
        x_rstd(0)
        x_squares(1)
        copy_head_gains()
        x_rstd(1)
        x_squares(2)
        x_rstd(2)
        x_squares(3)
        x_rstd(3)
        rope_tables()

        for a in range(TOKEN_TILES):
            normalise(a)
            transpose_h(a)
            group_h(a)
        regroup_weights(on_scalar, 1, 1, PIECE, PIECE)
        quantise_weights(0)
        quantise_h(0)
        quantise_h(1)
        regroup_weights(on_vector, 1, 0)
        quantise_h(2)
        regroup_weights(on_vector, 1, 1, 0, PIECE)
        quantise_h(3)
        regroup_weights(on_scalar, KEYS, 1)
        regroup_weights(on_vector, KEYS, 0)
        quantise_weights(1)
        regroup_weights(on_scalar, VALUES, 1)
        regroup_weights(on_vector, VALUES, 0)
        quantise_weights(KEYS)
        quantise_weights(VALUES)

        banks = [(c, a) for c in range(VALUES) for a in range(TOKEN_TILES)]
        project(*banks[0])
        head_squares(*banks[0], range(HEADS))
        for i, (c, a) in enumerate(banks):
            if i + 1 < len(banks):
                project(*banks[i + 1])
                head_squares(*banks[i + 1], range(1))
            head_rstd(c, a)
            if i + 1 < len(banks):
                head_squares(*banks[i + 1], range(1, HEADS))
            rotation_products(c, a, range(HEADS))
            if i + 1 < len(banks):
                add_products(nc.gpsimd, c, a, slice(0, HEADS))
                store(c, a)
            else:
                for first in (0, 2):
                    add_products(nc.vector, c, a, slice(first, first + 2))
                    store(c, a, first, 2)
            if 5 <= i < 9:
                project(VALUES, i - 5)
                copy_values(i - 5)
                store(VALUES, i - 5)
